import numpy as np
import ml_dtypes


def mxq(x, axis, fmt="e4m3"):
    dtype, down = {"e4m3": (ml_dtypes.float8_e4m3fn, 7), "e5m2": (ml_dtypes.float8_e5m2, 14)}[fmt]
    v = np.moveaxis(np.asarray(x, np.float32).astype(ml_dtypes.bfloat16).astype(np.float64), axis, -1)
    blocks = v.reshape(v.shape[:-1] + (-1, 32))
    amax = np.abs(blocks).max(-1, keepdims=True)
    byte = np.maximum(np.where(amax > 0, np.frexp(amax)[1] - 1 + 127, 0) - down, 1)
    scale = np.exp2(byte - 127.0)
    codes = (blocks / scale).astype(np.float32).astype(dtype).astype(np.float64)
    return np.moveaxis((codes * scale).reshape(v.shape), -1, axis)


WIDE = False


def mx_kscale(k):
    if not WIDE:
        return np.ones(k)
    levels = np.array([10, -10, 5, -5, 0])
    a = np.random.permutation(np.resize(levels, k // 512 * 4)).reshape(k // 512, 4)
    idx = np.arange(k)
    return np.exp2(a[idx // 512, idx % 128 // 32])


BF16 = ml_dtypes.bfloat16


def bf(x):
    return np.asarray(x, np.float32).astype(BF16)


def f64(x):
    return np.asarray(x).astype(np.float64)


B, D, M = 512, 1024, 4096
INPUT_FACTOR = 0.01
OUTPUT_FACTOR = 0.1


def setup_inputs():
    s = mx_kscale(D)
    s = s / s.max()
    inp = np.random.standard_normal((B, D)) * (np.sqrt(8.0 / D) / INPUT_FACTOR) * s
    h0 = np.random.standard_normal(M) * 0.5
    h = np.random.standard_normal((M, D)) * 0.5 / s
    p = np.random.standard_normal((M, D)) * np.sqrt(8.0 / D)
    p0 = np.random.standard_normal(M)
    pars = np.concatenate([h0, h.reshape(-1), p.reshape(-1), p0])
    return {"input": bf(inp), "pars": bf(pars)}


def _paraboloid(x, pars):
    h0 = pars[:M]
    h = pars[M:M + M * D].reshape(M, D)
    p = pars[M + M * D:M + 2 * M * D].reshape(M, D)
    p0 = pars[M + 2 * M * D:]
    xq = mxq(x, 1, "e4m3")
    hsum = (xq @ mxq(h, 1, "e4m3").T) + h0
    x_sq = np.sum(x * x, axis=-1, keepdims=True)
    p_sq = np.sum(p * p, axis=-1)
    dist_sq = x_sq - 2.0 * (xq @ mxq(p, 1, "e4m3").T) + p_sq
    return OUTPUT_FACTOR * (hsum * hsum - dist_sq + p0)


def reference(input, pars):
    x = INPUT_FACTOR * f64(input)
    return _paraboloid(x, f64(pars))

@@ -1,0 +1,243 @@
+import math
+from contextlib import ExitStack
+
+import concourse.mybir as mybir
+from concourse.masks import make_identity
+
+BF16 = mybir.dt.bfloat16
+F32 = mybir.dt.float32
+U32 = mybir.dt.uint32
+U8 = mybir.dt.uint8
+FP8X4 = mybir.dt.float8_e4m3fn_x4
+ALU = mybir.AluOpType
+ACT = mybir.ActivationFunctionType
+
+B, D, M = 512, 1024, 4096
+INPUT_FACTOR = 0.01
+OUTPUT_FACTOR = 0.1
+FLOPS = 2 * 2 * B * D * M
+
+P = 128
+PACK = 4
+PASSES = D // (P * PACK)
+WORDS = D // 2
+X_BLOCKS = B // P
+PAIRS = M // P
+
+ROOT_HALF = math.sqrt(0.5)
+ROOT_OUTPUT_FACTOR = math.sqrt(OUTPUT_FACTOR)
+
+MULTIPLY_LAG = 1
+COMBINE_LAG = 2
+BACK_LAG = 3
+PREFETCH = 8
+STORE_PAIRS = 4
+
+
+def tile_paraboloid_kernel(tc, inp, pars, out):
+    nc = tc.nc
+
+    h0_rows = pars[0:M].rearrange("(j m) -> j m", m=P)
+    h_blocks = pars[M : M + M * D].rearrange("(j m k) -> j m k", m=P, k=D)
+    p_blocks = pars[M + M * D : M + 2 * M * D].rearrange("(j m k) -> j m k", m=P, k=D)
+    p0_rows = pars[M + 2 * M * D : 2 * M + 2 * M * D].rearrange("(j m) -> j m", m=P)
+    x_blocks = inp.rearrange("(i b) k -> i b k", b=P)
+    out_view = out.rearrange("(i b) m -> b i m", b=P)
+
+    with ExitStack() as ctx:
+        consts = ctx.enter_context(tc.tile_pool(name="consts", bufs=1))
+        x_pool = ctx.enter_context(tc.tile_pool(name="x_raw", bufs=X_BLOCKS))
+        raw_pool = ctx.enter_context(tc.tile_pool(name="raw", bufs=2 * (PREFETCH + 1)))
+        mx_pool = ctx.enter_context(tc.tile_pool(name="mx", bufs=6))
+        work = ctx.enter_context(tc.tile_pool(name="work", bufs=2))
+        words_psum = ctx.enter_context(tc.psum_pool(name="words_psum", bufs=4))
+        acc_psum = ctx.enter_context(tc.psum_pool(name="acc_psum", bufs=1))
+        back_psum = ctx.enter_context(tc.psum_pool(name="back_psum", bufs=2))
+        ctx.enter_context(tc.manual_schedule())
+
+        def load_block(pool, rows):
+            raw = pool.tile([P, D], BF16)
+            nc.sync.dma_start(out=raw[:], in_=rows)
+            return raw
+
+        def transpose_words(raw):
+            words_t = words_psum.tile([P, WORDS], F32)
+            raw_words = raw[:].bitcast(F32)
+            for c in range(WORDS // P):
+                cols = slice(c * P, (c + 1) * P)
+                nc.tensor.transpose(words_t[:, cols], raw_words[:, cols], identity[:])
+            return words_t
+
+        def regroup(copy, words_t):
+            grouped = mx_pool.tile([P, D], BF16, align_bytes=64)
+            copy(
+                out=grouped[:].bitcast(F32).rearrange("q (g r u) -> q g r u", g=PASSES, u=2),
+                in_=words_t[:].rearrange("q (g u r) -> q g r u", g=PASSES, u=2),
+            )
+            return grouped
+
+        def quantise(grouped):
+            codes = mx_pool.tile([P, D // PACK], U32, align_bytes=64)
+            scales = mx_pool.tile([P, D // PACK], U8, align_bytes=64)
+            nc.vector.quantize_mx(out=codes[:].bitcast(FP8X4), scales=scales[:], in_=grouped[:])
+            return codes, scales
+
+        def multiply(acc, codes, scales):
+            for g in range(PASSES):
+                w_cols = slice(g * P, (g + 1) * P)
+                x_cols = slice(g * B, (g + 1) * B)
+                nc.tensor.matmul_mx(
+                    out=acc[:],
+                    lhsT=codes[:, w_cols].bitcast(FP8X4),
+                    lhsT_scale=scales[:, w_cols],
+                    rhs=x_codes[:, x_cols].bitcast(FP8X4),
+                    rhs_scale=x_scales[:, x_cols],
+                    start=(g == 0),
+                    stop=(g == PASSES - 1),
+                )
+
+        def sum_of_squares(raw, root_factor, total):
+            squares = work.tile([P, D], BF16)
+            nc.scalar.activation(
+                out=squares[:], in_=raw[:], func=ACT.Square, scale=root_factor, accum_out=total
+            )
+
+        identity = consts.tile([P, P], F32)
+        make_identity(nc, identity[:])
+
+        bias_rows = consts.tile([P, P], BF16)
+        nc.vector.memset(bias_rows[:], 0.0)
+        nc.scalar.dma_start(out=bias_rows[0:PAIRS, :], in_=h0_rows)
+        nc.scalar.dma_start(out=bias_rows[PAIRS : 2 * PAIRS, :], in_=p0_rows)
+
+        x_raw = [load_block(x_pool, x_blocks[i]) for i in range(X_BLOCKS)]
+        raw_h = {}
+        raw_p = {}
+        for j in range(PREFETCH):
+            raw_h[j] = load_block(raw_pool, h_blocks[j])
+            raw_p[j] = load_block(raw_pool, p_blocks[j])
+
+        x_grouped = consts.tile([P, PASSES * B * PACK], BF16, align_bytes=64)
+        x_codes = consts.tile([P, PASSES * B], U32, align_bytes=64)
+        x_scales = consts.tile([P, PASSES * B], U8, align_bytes=64)
+        x_grouped_view = x_grouped[:].rearrange("q (g b u e) -> q g b u e", g=PASSES, u=2, e=2)
+        for i in range(X_BLOCKS):
+            words_t = transpose_words(x_raw[i])
+            halves = words_t[:].bitcast(BF16).rearrange("q (g u r e) -> q g r u e", g=PASSES, u=2, e=2)
+            for g in range(PASSES):
+                dst = x_grouped_view[:, g, i * P : (i + 1) * P]
+                if i % 2 == 0:
+                    nc.vector.tensor_scalar_mul(out=dst, in0=halves[:, g], scalar1=INPUT_FACTOR)
+                else:
+                    nc.scalar.activation(out=dst, in_=halves[:, g], func=ACT.Copy, scale=INPUT_FACTOR)
+
+        bias_f32 = consts.tile([P, P], F32)
+        nc.vector.tensor_copy(out=bias_f32[:], in_=bias_rows[:])
+        bias_t = back_psum.tile([P, B], F32, tag="back")
+        nc.tensor.transpose(bias_t[:, 0:P], bias_f32[:], identity[:])
+
+        for g in range(PASSES):
+            nc.vector.quantize_mx(
+                out=x_codes[:, g * B : (g + 1) * B].bitcast(FP8X4),
+                scales=x_scales[:, g * B : (g + 1) * B],
+                in_=x_grouped[:, g * B * PACK : (g + 1) * B * PACK],
+            )
+
+        h0_bias = consts.tile([P, PAIRS], F32)
+        p0_half = consts.tile([P, PAIRS], F32)
+        nc.vector.tensor_scalar_mul(out=h0_bias[:], in0=bias_t[:, 0:PAIRS], scalar1=ROOT_HALF)
+        nc.vector.tensor_scalar_mul(out=p0_half[:], in0=bias_t[:, PAIRS : 2 * PAIRS], scalar1=0.5)
+
+        p_sq_half = consts.tile([P, PAIRS], F32)
+        p_term = consts.tile([P, PAIRS], F32)
+        x_term = consts.tile([P, X_BLOCKS], F32)
+
+        def neuron_term(j):
+            col = slice(j, j + 1)
+            sum_of_squares(raw_p[j], ROOT_HALF, p_sq_half[:, col])
+            nc.gpsimd.tensor_tensor(
+                out=p_term[:, col], in0=p0_half[:, col], in1=p_sq_half[:, col], op=ALU.subtract
+            )
+
+        def batch_term(i):
+            sum_of_squares(x_raw[i], INPUT_FACTOR * ROOT_OUTPUT_FACTOR, x_term[:, i : i + 1])
+
+        neuron_term(0)
+        batch_term(0)
+
+        words_h, words_p = {}, {}
+        grouped_h, grouped_p = {}, {}
+        mx_h, mx_p = {}, {}
+        product_p, half_square, combined, out_tiles = {}, {}, {}, {}
+
+        for r in range(PAIRS + BACK_LAG):
+            if r + PREFETCH < PAIRS:
+                raw_h[r + PREFETCH] = load_block(raw_pool, h_blocks[r + PREFETCH])
+                raw_p[r + PREFETCH] = load_block(raw_pool, p_blocks[r + PREFETCH])
+
+            j = r - COMBINE_LAG
+            if 0 <= j < PAIRS:
+                u = work.tile([P, B], F32)
+                nc.vector.scalar_tensor_tensor(
+                    out=u[:],
+                    in0=product_p[j][:],
+                    scalar=p_term[:, j : j + 1],
+                    in1=half_square[j][:],
+                    op0=ALU.add,
+                    op1=ALU.add,
+                )
+                combined[j] = u
+
+            if r < PAIRS:
+                words_h[r] = transpose_words(raw_h[r])
+                words_p[r] = transpose_words(raw_p[r])
+            j = r - BACK_LAG
+            if 0 <= j < PAIRS:
+                back = back_psum.tile([P, B], F32)
+                for i in range(X_BLOCKS):
+                    cols = slice(i * P, (i + 1) * P)
+                    nc.tensor.transpose(back[:, cols], combined[j][:, cols], identity[:])
+
+            if r < PAIRS:
+                grouped_h[r] = regroup(nc.vector.tensor_copy, words_h[r])
+                grouped_p[r] = regroup(nc.scalar.copy, words_p[r])
+
+            if 0 <= j < PAIRS:
+                if j % STORE_PAIRS == 0:
+                    out_sb = work.tile([P, X_BLOCKS, STORE_PAIRS * P], F32)
+                    out_tiles[j // STORE_PAIRS] = out_sb
+                out_sb = out_tiles[j // STORE_PAIRS]
+                first = (j % STORE_PAIRS) * P
+                nc.vector.scalar_tensor_tensor(
+                    out=out_sb[:, :, first : first + P],
+                    in0=back[:].rearrange("b (i m) -> b i m", i=X_BLOCKS),
+                    scalar=2.0 * OUTPUT_FACTOR,
+                    in1=x_term[:].unsqueeze(2).to_broadcast([P, X_BLOCKS, P]),
+                    op0=ALU.mult,
+                    op1=ALU.subtract,
+                )
+                if j % STORE_PAIRS == STORE_PAIRS - 1:
+                    last = (j + 1) * P
+                    nc.sync.dma_start(out=out_view[:, :, last - STORE_PAIRS * P : last], in_=out_sb[:])
+
+            if r < PAIRS:
+                mx_h[r] = quantise(grouped_h[r])
+                mx_p[r] = quantise(grouped_p[r])
+
+            j = r - MULTIPLY_LAG
+            if 0 <= j < PAIRS:
+                acc_h = acc_psum.tile([P, B], F32)
+                acc_p = acc_psum.tile([P, B], F32)
+                multiply(acc_h, mx_h[j][0], mx_h[j][1])
+                multiply(acc_p, mx_p[j][0], mx_p[j][1])
+                product_p[j] = acc_p
+                s = work.tile([P, B], F32)
+                nc.scalar.activation(
+                    out=s[:], in_=acc_h[:], func=ACT.Square, bias=h0_bias[:, j : j + 1], scale=ROOT_HALF
+                )
+                half_square[j] = s
+
+            if r + 1 < PAIRS:
+                neuron_term(r + 1)
+            if r + 1 < X_BLOCKS:
+                batch_term(r + 1)

@@ -27,11 +27,12 @@ PAIRS = M // P
 ROOT_HALF = math.sqrt(0.5)
 ROOT_OUTPUT_FACTOR = math.sqrt(OUTPUT_FACTOR)
 
+PAIRS_PER_ROUND = 2
+ROUNDS = PAIRS // PAIRS_PER_ROUND
 MULTIPLY_LAG = 1
-COMBINE_LAG = 2
-BACK_LAG = 3
-PREFETCH = 8
-STORE_PAIRS = 4
+FINISH_LAG = 2
+PREFETCH = 4
+PSUM_BANKS = 8
 
 
 def tile_paraboloid_kernel(tc, inp, pars, out):
@@ -47,12 +48,12 @@ def tile_paraboloid_kernel(tc, inp, pars, out):
     with ExitStack() as ctx:
         consts = ctx.enter_context(tc.tile_pool(name="consts", bufs=1))
         x_pool = ctx.enter_context(tc.tile_pool(name="x_raw", bufs=X_BLOCKS))
-        raw_pool = ctx.enter_context(tc.tile_pool(name="raw", bufs=2 * (PREFETCH + 1)))
-        mx_pool = ctx.enter_context(tc.tile_pool(name="mx", bufs=6))
-        work = ctx.enter_context(tc.tile_pool(name="work", bufs=2))
-        words_psum = ctx.enter_context(tc.psum_pool(name="words_psum", bufs=4))
-        acc_psum = ctx.enter_context(tc.psum_pool(name="acc_psum", bufs=1))
-        back_psum = ctx.enter_context(tc.psum_pool(name="back_psum", bufs=2))
+        raw_pool = ctx.enter_context(
+            tc.tile_pool(name="raw", bufs=2 * PAIRS_PER_ROUND * (PREFETCH + 1))
+        )
+        mx_pool = ctx.enter_context(tc.tile_pool(name="mx", bufs=2 * 2 * PAIRS_PER_ROUND))
+        work = ctx.enter_context(tc.tile_pool(name="work", bufs=2 * PAIRS_PER_ROUND))
+        psum = ctx.enter_context(tc.psum_pool(name="psum", bufs=PSUM_BANKS))
         ctx.enter_context(tc.manual_schedule())
 
         def load_block(pool, rows):
@@ -61,7 +62,7 @@ def tile_paraboloid_kernel(tc, inp, pars, out):
             return raw
 
         def transpose_words(raw):
-            words_t = words_psum.tile([P, WORDS], F32)
+            words_t = psum.tile([P, WORDS], F32, tag="bank")
             raw_words = raw[:].bitcast(F32)
             for c in range(WORDS // P):
                 cols = slice(c * P, (c + 1) * P)
@@ -113,7 +114,7 @@ def tile_paraboloid_kernel(tc, inp, pars, out):
         x_raw = [load_block(x_pool, x_blocks[i]) for i in range(X_BLOCKS)]
         raw_h = {}
         raw_p = {}
-        for j in range(PREFETCH):
+        for j in range(PREFETCH * PAIRS_PER_ROUND):
             raw_h[j] = load_block(raw_pool, h_blocks[j])
             raw_p[j] = load_block(raw_pool, p_blocks[j])
 
@@ -133,7 +134,7 @@ def tile_paraboloid_kernel(tc, inp, pars, out):
 
         bias_f32 = consts.tile([P, P], F32)
         nc.vector.tensor_copy(out=bias_f32[:], in_=bias_rows[:])
-        bias_t = back_psum.tile([P, B], F32, tag="back")
+        bias_t = psum.tile([P, B], F32, tag="bank")
         nc.tensor.transpose(bias_t[:, 0:P], bias_f32[:], identity[:])
 
         for g in range(PASSES):
@@ -162,21 +163,23 @@ def tile_paraboloid_kernel(tc, inp, pars, out):
         def batch_term(i):
             sum_of_squares(x_raw[i], INPUT_FACTOR * ROOT_OUTPUT_FACTOR, x_term[:, i : i + 1])
 
-        neuron_term(0)
-        batch_term(0)
 
         words_h, words_p = {}, {}
         grouped_h, grouped_p = {}, {}
         mx_h, mx_p = {}, {}
-        product_p, half_square, combined, out_tiles = {}, {}, {}, {}
+        product_h, product_p, half_square, combined, transposed = {}, {}, {}, {}, {}
 
-        for r in range(PAIRS + BACK_LAG):
-            if r + PREFETCH < PAIRS:
-                raw_h[r + PREFETCH] = load_block(raw_pool, h_blocks[r + PREFETCH])
-                raw_p[r + PREFETCH] = load_block(raw_pool, p_blocks[r + PREFETCH])
+        def pairs_of(t):
+            if 0 <= t < ROUNDS:
+                return range(t * PAIRS_PER_ROUND, (t + 1) * PAIRS_PER_ROUND)
+            return range(0)
 
-            j = r - COMBINE_LAG
-            if 0 <= j < PAIRS:
+        for t in range(ROUNDS + FINISH_LAG):
+            for j in pairs_of(t + PREFETCH):
+                raw_h[j] = load_block(raw_pool, h_blocks[j])
+                raw_p[j] = load_block(raw_pool, p_blocks[j])
+
+            for j in pairs_of(t - FINISH_LAG):
                 u = work.tile([P, B], F32)
                 nc.vector.scalar_tensor_tensor(
                     out=u[:],
@@ -188,56 +191,60 @@ def tile_paraboloid_kernel(tc, inp, pars, out):
                 )
                 combined[j] = u
 
-            if r < PAIRS:
-                words_h[r] = transpose_words(raw_h[r])
-                words_p[r] = transpose_words(raw_p[r])
-            j = r - BACK_LAG
-            if 0 <= j < PAIRS:
-                back = back_psum.tile([P, B], F32)
+            for j in pairs_of(t):
+                words_h[j] = transpose_words(raw_h[j])
+                words_p[j] = transpose_words(raw_p[j])
+            for j in pairs_of(t - FINISH_LAG):
+                u_t = psum.tile([P, B], F32, tag="bank")
                 for i in range(X_BLOCKS):
                     cols = slice(i * P, (i + 1) * P)
-                    nc.tensor.transpose(back[:, cols], combined[j][:, cols], identity[:])
+                    nc.tensor.transpose(u_t[:, cols], combined[j][:, cols], identity[:])
+                transposed[j] = u_t
 
-            if r < PAIRS:
-                grouped_h[r] = regroup(nc.vector.tensor_copy, words_h[r])
-                grouped_p[r] = regroup(nc.scalar.copy, words_p[r])
+            for j in pairs_of(t):
+                grouped_h[j] = regroup(nc.vector.tensor_copy, words_h[j])
+                grouped_p[j] = regroup(nc.scalar.copy, words_p[j])
 
-            if 0 <= j < PAIRS:
-                if j % STORE_PAIRS == 0:
-                    out_sb = work.tile([P, X_BLOCKS, STORE_PAIRS * P], F32)
-                    out_tiles[j // STORE_PAIRS] = out_sb
-                out_sb = out_tiles[j // STORE_PAIRS]
-                first = (j % STORE_PAIRS) * P
-                nc.vector.scalar_tensor_tensor(
-                    out=out_sb[:, :, first : first + P],
-                    in0=back[:].rearrange("b (i m) -> b i m", i=X_BLOCKS),
-                    scalar=2.0 * OUTPUT_FACTOR,
-                    in1=x_term[:].unsqueeze(2).to_broadcast([P, X_BLOCKS, P]),
-                    op0=ALU.mult,
-                    op1=ALU.subtract,
+            if 0 <= t - FINISH_LAG:
+                out_sb = work.tile([P, X_BLOCKS, PAIRS_PER_ROUND * P], F32)
+                for n, j in enumerate(pairs_of(t - FINISH_LAG)):
+                    nc.vector.scalar_tensor_tensor(
+                        out=out_sb[:, :, n * P : (n + 1) * P],
+                        in0=transposed[j][:].rearrange("b (i m) -> b i m", i=X_BLOCKS),
+                        scalar=2.0 * OUTPUT_FACTOR,
+                        in1=x_term[:].unsqueeze(2).to_broadcast([P, X_BLOCKS, P]),
+                        op0=ALU.mult,
+                        op1=ALU.subtract,
+                    )
+                first = (t - FINISH_LAG) * PAIRS_PER_ROUND * P
+                nc.sync.dma_start(
+                    out=out_view[:, :, first : first + PAIRS_PER_ROUND * P], in_=out_sb[:]
                 )
-                if j % STORE_PAIRS == STORE_PAIRS - 1:
-                    last = (j + 1) * P
-                    nc.sync.dma_start(out=out_view[:, :, last - STORE_PAIRS * P : last], in_=out_sb[:])
 
-            if r < PAIRS:
-                mx_h[r] = quantise(grouped_h[r])
-                mx_p[r] = quantise(grouped_p[r])
+            for j in pairs_of(t):
+                mx_h[j] = quantise(grouped_h[j])
+                mx_p[j] = quantise(grouped_p[j])
 
-            j = r - MULTIPLY_LAG
-            if 0 <= j < PAIRS:
-                acc_h = acc_psum.tile([P, B], F32)
-                acc_p = acc_psum.tile([P, B], F32)
+            for j in pairs_of(t - MULTIPLY_LAG):
+                acc_h = psum.tile([P, B], F32, tag="bank")
                 multiply(acc_h, mx_h[j][0], mx_h[j][1])
+                product_h[j] = acc_h
+                acc_p = psum.tile([P, B], F32, tag="bank")
                 multiply(acc_p, mx_p[j][0], mx_p[j][1])
                 product_p[j] = acc_p
+            for j in pairs_of(t - MULTIPLY_LAG):
                 s = work.tile([P, B], F32)
                 nc.scalar.activation(
-                    out=s[:], in_=acc_h[:], func=ACT.Square, bias=h0_bias[:, j : j + 1], scale=ROOT_HALF
+                    out=s[:],
+                    in_=product_h[j][:],
+                    func=ACT.Square,
+                    bias=h0_bias[:, j : j + 1],
+                    scale=ROOT_HALF,
                 )
                 half_square[j] = s
 
-            if r + 1 < PAIRS:
-                neuron_term(r + 1)
-            if r + 1 < X_BLOCKS:
-                batch_term(r + 1)
+            for j in pairs_of(t):
+                neuron_term(j)
+            for i in range(X_BLOCKS):
+                if i // (X_BLOCKS // FINISH_LAG) == t:
+                    batch_term(i)

@@ -27,12 +27,10 @@ PAIRS = M // P
 ROOT_HALF = math.sqrt(0.5)
 ROOT_OUTPUT_FACTOR = math.sqrt(OUTPUT_FACTOR)
 
-PAIRS_PER_ROUND = 2
-ROUNDS = PAIRS // PAIRS_PER_ROUND
 MULTIPLY_LAG = 1
-FINISH_LAG = 2
-PREFETCH = 4
-PSUM_BANKS = 8
+COMBINE_LAG = 2
+BACK_LAG = 3
+PREFETCH = 8
 
 
 def tile_paraboloid_kernel(tc, inp, pars, out):
@@ -48,12 +46,13 @@ def tile_paraboloid_kernel(tc, inp, pars, out):
     with ExitStack() as ctx:
         consts = ctx.enter_context(tc.tile_pool(name="consts", bufs=1))
         x_pool = ctx.enter_context(tc.tile_pool(name="x_raw", bufs=X_BLOCKS))
-        raw_pool = ctx.enter_context(
-            tc.tile_pool(name="raw", bufs=2 * PAIRS_PER_ROUND * (PREFETCH + 1))
-        )
-        mx_pool = ctx.enter_context(tc.tile_pool(name="mx", bufs=2 * 2 * PAIRS_PER_ROUND))
-        work = ctx.enter_context(tc.tile_pool(name="work", bufs=2 * PAIRS_PER_ROUND))
-        psum = ctx.enter_context(tc.psum_pool(name="psum", bufs=PSUM_BANKS))
+        raw_pool = ctx.enter_context(tc.tile_pool(name="raw", bufs=2 * (PREFETCH + 1)))
+        mx_pool = ctx.enter_context(tc.tile_pool(name="mx", bufs=6))
+        work = ctx.enter_context(tc.tile_pool(name="work", bufs=2))
+        out_pool = ctx.enter_context(tc.tile_pool(name="out", bufs=4))
+        words_psum = ctx.enter_context(tc.psum_pool(name="words_psum", bufs=4))
+        acc_psum = ctx.enter_context(tc.psum_pool(name="acc_psum", bufs=1))
+        back_psum = ctx.enter_context(tc.psum_pool(name="back_psum", bufs=2))
         ctx.enter_context(tc.manual_schedule())
 
         def load_block(pool, rows):
@@ -62,19 +61,19 @@ def tile_paraboloid_kernel(tc, inp, pars, out):
             return raw
 
         def transpose_words(raw):
-            words_t = psum.tile([P, WORDS], F32, tag="bank")
+            words_t = words_psum.tile([P, WORDS], F32)
             raw_words = raw[:].bitcast(F32)
             for c in range(WORDS // P):
                 cols = slice(c * P, (c + 1) * P)
                 nc.tensor.transpose(words_t[:, cols], raw_words[:, cols], identity[:])
             return words_t
 
-        def regroup(copy, words_t):
+        def regroup(copy, words_t, grouped_words):
+            copy(out=grouped_words, in_=words_t[:].rearrange("q (g u r) -> q g r u", g=PASSES, u=2))
+
+        def regroup_block(copy, words_t):
             grouped = mx_pool.tile([P, D], BF16, align_bytes=64)
-            copy(
-                out=grouped[:].bitcast(F32).rearrange("q (g r u) -> q g r u", g=PASSES, u=2),
-                in_=words_t[:].rearrange("q (g u r) -> q g r u", g=PASSES, u=2),
-            )
+            regroup(copy, words_t, grouped[:].bitcast(F32).rearrange("q (g r u) -> q g r u", g=PASSES, u=2))
             return grouped
 
         def quantise(grouped):
@@ -114,29 +113,29 @@ def tile_paraboloid_kernel(tc, inp, pars, out):
         x_raw = [load_block(x_pool, x_blocks[i]) for i in range(X_BLOCKS)]
         raw_h = {}
         raw_p = {}
-        for j in range(PREFETCH * PAIRS_PER_ROUND):
+        for j in range(PREFETCH):
             raw_h[j] = load_block(raw_pool, h_blocks[j])
             raw_p[j] = load_block(raw_pool, p_blocks[j])
 
+        x_term = consts.tile([P, X_BLOCKS], F32)
+        inp_grouped = consts.tile([P, PASSES * B * PACK], BF16)
         x_grouped = consts.tile([P, PASSES * B * PACK], BF16, align_bytes=64)
         x_codes = consts.tile([P, PASSES * B], U32, align_bytes=64)
         x_scales = consts.tile([P, PASSES * B], U8, align_bytes=64)
-        x_grouped_view = x_grouped[:].rearrange("q (g b u e) -> q g b u e", g=PASSES, u=2, e=2)
+        inp_grouped_words = inp_grouped[:].bitcast(F32).rearrange("q (g b u) -> q g b u", g=PASSES, u=2)
         for i in range(X_BLOCKS):
+            sum_of_squares(x_raw[i], INPUT_FACTOR * ROOT_OUTPUT_FACTOR, x_term[:, i : i + 1])
             words_t = transpose_words(x_raw[i])
-            halves = words_t[:].bitcast(BF16).rearrange("q (g u r e) -> q g r u e", g=PASSES, u=2, e=2)
-            for g in range(PASSES):
-                dst = x_grouped_view[:, g, i * P : (i + 1) * P]
-                if i % 2 == 0:
-                    nc.vector.tensor_scalar_mul(out=dst, in0=halves[:, g], scalar1=INPUT_FACTOR)
-                else:
-                    nc.scalar.activation(out=dst, in_=halves[:, g], func=ACT.Copy, scale=INPUT_FACTOR)
+            regroup(nc.vector.tensor_copy, words_t, inp_grouped_words[:, :, i * P : (i + 1) * P, :])
 
         bias_f32 = consts.tile([P, P], F32)
         nc.vector.tensor_copy(out=bias_f32[:], in_=bias_rows[:])
-        bias_t = psum.tile([P, B], F32, tag="bank")
+        bias_t = back_psum.tile([P, B], F32, tag="back")
         nc.tensor.transpose(bias_t[:, 0:P], bias_f32[:], identity[:])
 
+        for g in range(PASSES):
+            cols = slice(g * B * PACK, (g + 1) * B * PACK)
+            nc.vector.tensor_scalar_mul(out=x_grouped[:, cols], in0=inp_grouped[:, cols], scalar1=INPUT_FACTOR)
         for g in range(PASSES):
             nc.vector.quantize_mx(
                 out=x_codes[:, g * B : (g + 1) * B].bitcast(FP8X4),
@@ -151,7 +150,6 @@ def tile_paraboloid_kernel(tc, inp, pars, out):
 
         p_sq_half = consts.tile([P, PAIRS], F32)
         p_term = consts.tile([P, PAIRS], F32)
-        x_term = consts.tile([P, X_BLOCKS], F32)
 
         def neuron_term(j):
             col = slice(j, j + 1)
@@ -160,26 +158,18 @@ def tile_paraboloid_kernel(tc, inp, pars, out):
                 out=p_term[:, col], in0=p0_half[:, col], in1=p_sq_half[:, col], op=ALU.subtract
             )
 
-        def batch_term(i):
-            sum_of_squares(x_raw[i], INPUT_FACTOR * ROOT_OUTPUT_FACTOR, x_term[:, i : i + 1])
-
-
         words_h, words_p = {}, {}
         grouped_h, grouped_p = {}, {}
         mx_h, mx_p = {}, {}
-        product_h, product_p, half_square, combined, transposed = {}, {}, {}, {}, {}
+        product_p, half_square, combined = {}, {}, {}
 
-        def pairs_of(t):
-            if 0 <= t < ROUNDS:
-                return range(t * PAIRS_PER_ROUND, (t + 1) * PAIRS_PER_ROUND)
-            return range(0)
+        for r in range(PAIRS + BACK_LAG):
+            if r + PREFETCH < PAIRS:
+                raw_h[r + PREFETCH] = load_block(raw_pool, h_blocks[r + PREFETCH])
+                raw_p[r + PREFETCH] = load_block(raw_pool, p_blocks[r + PREFETCH])
 
-        for t in range(ROUNDS + FINISH_LAG):
-            for j in pairs_of(t + PREFETCH):
-                raw_h[j] = load_block(raw_pool, h_blocks[j])
-                raw_p[j] = load_block(raw_pool, p_blocks[j])
-
-            for j in pairs_of(t - FINISH_LAG):
+            j = r - COMBINE_LAG
+            if 0 <= j < PAIRS:
                 u = work.tile([P, B], F32)
                 nc.vector.scalar_tensor_tensor(
                     out=u[:],
@@ -191,60 +181,48 @@ def tile_paraboloid_kernel(tc, inp, pars, out):
                 )
                 combined[j] = u
 
-            for j in pairs_of(t):
-                words_h[j] = transpose_words(raw_h[j])
-                words_p[j] = transpose_words(raw_p[j])
-            for j in pairs_of(t - FINISH_LAG):
-                u_t = psum.tile([P, B], F32, tag="bank")
+            if r < PAIRS:
+                words_h[r] = transpose_words(raw_h[r])
+                words_p[r] = transpose_words(raw_p[r])
+            j = r - BACK_LAG
+            if 0 <= j < PAIRS:
+                back = back_psum.tile([P, B], F32)
                 for i in range(X_BLOCKS):
                     cols = slice(i * P, (i + 1) * P)
-                    nc.tensor.transpose(u_t[:, cols], combined[j][:, cols], identity[:])
-                transposed[j] = u_t
+                    nc.tensor.transpose(back[:, cols], combined[j][:, cols], identity[:])
 
-            for j in pairs_of(t):
-                grouped_h[j] = regroup(nc.vector.tensor_copy, words_h[j])
-                grouped_p[j] = regroup(nc.scalar.copy, words_p[j])
+            if r < PAIRS:
+                grouped_h[r] = regroup_block(nc.vector.tensor_copy, words_h[r])
+                grouped_p[r] = regroup_block(nc.scalar.copy, words_p[r])
 
-            if 0 <= t - FINISH_LAG:
-                out_sb = work.tile([P, X_BLOCKS, PAIRS_PER_ROUND * P], F32)
-                for n, j in enumerate(pairs_of(t - FINISH_LAG)):
-                    nc.vector.scalar_tensor_tensor(
-                        out=out_sb[:, :, n * P : (n + 1) * P],
-                        in0=transposed[j][:].rearrange("b (i m) -> b i m", i=X_BLOCKS),
-                        scalar=2.0 * OUTPUT_FACTOR,
-                        in1=x_term[:].unsqueeze(2).to_broadcast([P, X_BLOCKS, P]),
-                        op0=ALU.mult,
-                        op1=ALU.subtract,
-                    )
-                first = (t - FINISH_LAG) * PAIRS_PER_ROUND * P
-                nc.sync.dma_start(
-                    out=out_view[:, :, first : first + PAIRS_PER_ROUND * P], in_=out_sb[:]
+            if 0 <= j < PAIRS:
+                out_sb = out_pool.tile([P, X_BLOCKS, P], F32)
+                nc.vector.scalar_tensor_tensor(
+                    out=out_sb[:],
+                    in0=back[:].rearrange("b (i m) -> b i m", i=X_BLOCKS),
+                    scalar=2.0 * OUTPUT_FACTOR,
+                    in1=x_term[:].unsqueeze(2).to_broadcast([P, X_BLOCKS, P]),
+                    op0=ALU.mult,
+                    op1=ALU.subtract,
                 )
+                nc.sync.dma_start(out=out_view[:, :, j * P : (j + 1) * P], in_=out_sb[:])
 
-            for j in pairs_of(t):
-                mx_h[j] = quantise(grouped_h[j])
-                mx_p[j] = quantise(grouped_p[j])
+            if r < PAIRS:
+                mx_h[r] = quantise(grouped_h[r])
+                mx_p[r] = quantise(grouped_p[r])
 
-            for j in pairs_of(t - MULTIPLY_LAG):
-                acc_h = psum.tile([P, B], F32, tag="bank")
+            j = r - MULTIPLY_LAG
+            if 0 <= j < PAIRS:
+                acc_h = acc_psum.tile([P, B], F32)
+                acc_p = acc_psum.tile([P, B], F32)
                 multiply(acc_h, mx_h[j][0], mx_h[j][1])
-                product_h[j] = acc_h
-                acc_p = psum.tile([P, B], F32, tag="bank")
                 multiply(acc_p, mx_p[j][0], mx_p[j][1])
                 product_p[j] = acc_p
-            for j in pairs_of(t - MULTIPLY_LAG):
                 s = work.tile([P, B], F32)
                 nc.scalar.activation(
-                    out=s[:],
-                    in_=product_h[j][:],
-                    func=ACT.Square,
-                    bias=h0_bias[:, j : j + 1],
-                    scale=ROOT_HALF,
+                    out=s[:], in_=acc_h[:], func=ACT.Square, bias=h0_bias[:, j : j + 1], scale=ROOT_HALF
                 )
                 half_square[j] = s
 
-            for j in pairs_of(t):
-                neuron_term(j)
-            for i in range(X_BLOCKS):
-                if i // (X_BLOCKS // FINISH_LAG) == t:
-                    batch_term(i)
+            if r < PAIRS:
+                neuron_term(r)

@@ -118,24 +118,25 @@ def tile_paraboloid_kernel(tc, inp, pars, out):
             raw_p[j] = load_block(raw_pool, p_blocks[j])
 
         x_term = consts.tile([P, X_BLOCKS], F32)
-        inp_grouped = consts.tile([P, PASSES * B * PACK], BF16)
         x_grouped = consts.tile([P, PASSES * B * PACK], BF16, align_bytes=64)
         x_codes = consts.tile([P, PASSES * B], U32, align_bytes=64)
         x_scales = consts.tile([P, PASSES * B], U8, align_bytes=64)
-        inp_grouped_words = inp_grouped[:].bitcast(F32).rearrange("q (g b u) -> q g b u", g=PASSES, u=2)
+        x_grouped_view = x_grouped[:].rearrange("q (g b u e) -> q g b u e", g=PASSES, u=2, e=2)
         for i in range(X_BLOCKS):
             sum_of_squares(x_raw[i], INPUT_FACTOR * ROOT_OUTPUT_FACTOR, x_term[:, i : i + 1])
             words_t = transpose_words(x_raw[i])
-            regroup(nc.vector.tensor_copy, words_t, inp_grouped_words[:, :, i * P : (i + 1) * P, :])
+            for g in range(PASSES):
+                nc.vector.tensor_scalar_mul(
+                    out=x_grouped_view[:, g, i * P : (i + 1) * P],
+                    in0=words_t[:].bitcast(BF16).rearrange("q (g u r e) -> q g r u e", g=PASSES, u=2, e=2)[:, g],
+                    scalar1=INPUT_FACTOR,
+                )
 
         bias_f32 = consts.tile([P, P], F32)
         nc.vector.tensor_copy(out=bias_f32[:], in_=bias_rows[:])
         bias_t = back_psum.tile([P, B], F32, tag="back")
         nc.tensor.transpose(bias_t[:, 0:P], bias_f32[:], identity[:])
 
-        for g in range(PASSES):
-            cols = slice(g * B * PACK, (g + 1) * B * PACK)
-            nc.vector.tensor_scalar_mul(out=x_grouped[:, cols], in0=inp_grouped[:, cols], scalar1=INPUT_FACTOR)
         for g in range(PASSES):
             nc.vector.quantize_mx(
                 out=x_codes[:, g * B : (g + 1) * B].bitcast(FP8X4),

@@ -102,11 +102,17 @@ def tile_paraboloid_kernel(tc, inp, pars, out):
                 out=squares[:], in_=raw[:], func=ACT.Square, scale=root_factor, accum_out=total
             )
 
+        def sum_of_squares_on_vector(raw, factor, total):
+            squares = work.tile([P, D], BF16)
+            nc.vector.scalar_tensor_tensor(
+                out=squares[:], in0=raw[:], scalar=factor, in1=raw[:], op0=ALU.mult, op1=ALU.mult, accum_out=total
+            )
+
         identity = consts.tile([P, P], F32)
         make_identity(nc, identity[:])
 
         bias_rows = consts.tile([P, P], BF16)
-        nc.vector.memset(bias_rows[:], 0.0)
+        nc.vector.memset(bias_rows[2 * PAIRS : P, :], 0.0)
         nc.scalar.dma_start(out=bias_rows[0:PAIRS, :], in_=h0_rows)
         nc.scalar.dma_start(out=bias_rows[PAIRS : 2 * PAIRS, :], in_=p0_rows)
 
@@ -117,13 +123,20 @@ def tile_paraboloid_kernel(tc, inp, pars, out):
             raw_h[j] = load_block(raw_pool, h_blocks[j])
             raw_p[j] = load_block(raw_pool, p_blocks[j])
 
+        bias_f32 = consts.tile([P, P], F32)
+        nc.vector.tensor_copy(out=bias_f32[:], in_=bias_rows[:])
+
         x_term = consts.tile([P, X_BLOCKS], F32)
         x_grouped = consts.tile([P, PASSES * B * PACK], BF16, align_bytes=64)
         x_codes = consts.tile([P, PASSES * B], U32, align_bytes=64)
         x_scales = consts.tile([P, PASSES * B], U8, align_bytes=64)
         x_grouped_view = x_grouped[:].rearrange("q (g b u e) -> q g b u e", g=PASSES, u=2, e=2)
+
         for i in range(X_BLOCKS):
-            sum_of_squares(x_raw[i], INPUT_FACTOR * ROOT_OUTPUT_FACTOR, x_term[:, i : i + 1])
+            if i == 0:
+                sum_of_squares_on_vector(x_raw[i], OUTPUT_FACTOR * INPUT_FACTOR**2, x_term[:, i : i + 1])
+            else:
+                sum_of_squares(x_raw[i], INPUT_FACTOR * ROOT_OUTPUT_FACTOR, x_term[:, i : i + 1])
             words_t = transpose_words(x_raw[i])
             for g in range(PASSES):
                 nc.vector.tensor_scalar_mul(
@@ -132,8 +145,6 @@ def tile_paraboloid_kernel(tc, inp, pars, out):
                     scalar1=INPUT_FACTOR,
                 )
 
-        bias_f32 = consts.tile([P, P], F32)
-        nc.vector.tensor_copy(out=bias_f32[:], in_=bias_rows[:])
         bias_t = back_psum.tile([P, B], F32, tag="back")
         nc.tensor.transpose(bias_t[:, 0:P], bias_f32[:], identity[:])
 
@@ -146,8 +157,6 @@ def tile_paraboloid_kernel(tc, inp, pars, out):
 
         h0_bias = consts.tile([P, PAIRS], F32)
         p0_half = consts.tile([P, PAIRS], F32)
-        nc.vector.tensor_scalar_mul(out=h0_bias[:], in0=bias_t[:, 0:PAIRS], scalar1=ROOT_HALF)
-        nc.vector.tensor_scalar_mul(out=p0_half[:], in0=bias_t[:, PAIRS : 2 * PAIRS], scalar1=0.5)
 
         p_sq_half = consts.tile([P, PAIRS], F32)
         p_term = consts.tile([P, PAIRS], F32)
@@ -193,7 +202,7 @@ def tile_paraboloid_kernel(tc, inp, pars, out):
                     nc.tensor.transpose(back[:, cols], combined[j][:, cols], identity[:])
 
             if r < PAIRS:
-                grouped_h[r] = regroup_block(nc.vector.tensor_copy, words_h[r])
+                grouped_h[r] = regroup_block(nc.scalar.copy if r == 0 else nc.vector.tensor_copy, words_h[r])
                 grouped_p[r] = regroup_block(nc.scalar.copy, words_p[r])
 
             if 0 <= j < PAIRS:
@@ -211,6 +220,9 @@ def tile_paraboloid_kernel(tc, inp, pars, out):
             if r < PAIRS:
                 mx_h[r] = quantise(grouped_h[r])
                 mx_p[r] = quantise(grouped_p[r])
+            if r == 0:
+                nc.vector.tensor_scalar_mul(out=h0_bias[:], in0=bias_t[:, 0:PAIRS], scalar1=ROOT_HALF)
+                nc.vector.tensor_scalar_mul(out=p0_half[:], in0=bias_t[:, PAIRS : 2 * PAIRS], scalar1=0.5)
 
             j = r - MULTIPLY_LAG
             if 0 <= j < PAIRS:

@@ -110,9 +110,17 @@ def tile_paraboloid_kernel(tc, inp, pars, out):
 
         identity = consts.tile([P, P], F32)
         make_identity(nc, identity[:])
+        zeros = consts.tile([P, B], BF16)
+        nc.vector.memset(zeros[:], 0.0)
+        warm_bank = back_psum.tile([P, B], F32, tag="back")
+
+        def keep_busy(count):
+            for i in range(count):
+                nc.tensor.matmul(warm_bank[:], zeros[:, 0:P], zeros[:], start=True, stop=True)
+
+        keep_busy(4)
 
         bias_rows = consts.tile([P, P], BF16)
-        nc.vector.memset(bias_rows[2 * PAIRS : P, :], 0.0)
         nc.scalar.dma_start(out=bias_rows[0:PAIRS, :], in_=h0_rows)
         nc.scalar.dma_start(out=bias_rows[PAIRS : 2 * PAIRS, :], in_=p0_rows)
 
@@ -124,7 +132,9 @@ def tile_paraboloid_kernel(tc, inp, pars, out):
             raw_p[j] = load_block(raw_pool, p_blocks[j])
 
         bias_f32 = consts.tile([P, P], F32)
-        nc.vector.tensor_copy(out=bias_f32[:], in_=bias_rows[:])
+        nc.vector.memset(bias_f32[2 * PAIRS : P, :], 0.0)
+        for rows, factor in ((slice(0, PAIRS), ROOT_HALF), (slice(PAIRS, 2 * PAIRS), 0.5)):
+            nc.vector.tensor_scalar_mul(out=bias_f32[rows, :], in0=bias_rows[rows, :], scalar1=factor)
 
         x_term = consts.tile([P, X_BLOCKS], F32)
         x_grouped = consts.tile([P, PASSES * B * PACK], BF16, align_bytes=64)
@@ -138,6 +148,8 @@ def tile_paraboloid_kernel(tc, inp, pars, out):
             else:
                 sum_of_squares(x_raw[i], INPUT_FACTOR * ROOT_OUTPUT_FACTOR, x_term[:, i : i + 1])
             words_t = transpose_words(x_raw[i])
+            if i < X_BLOCKS - 1:
+                keep_busy(1)
             for g in range(PASSES):
                 nc.vector.tensor_scalar_mul(
                     out=x_grouped_view[:, g, i * P : (i + 1) * P],
@@ -155,8 +167,9 @@ def tile_paraboloid_kernel(tc, inp, pars, out):
                 in_=x_grouped[:, g * B * PACK : (g + 1) * B * PACK],
             )
 
-        h0_bias = consts.tile([P, PAIRS], F32)
-        p0_half = consts.tile([P, PAIRS], F32)
+        bias_columns = consts.tile([P, 2 * PAIRS], F32)
+        h0_bias = bias_columns[:, 0:PAIRS]
+        p0_half = bias_columns[:, PAIRS : 2 * PAIRS]
 
         p_sq_half = consts.tile([P, PAIRS], F32)
         p_term = consts.tile([P, PAIRS], F32)
@@ -167,6 +180,43 @@ def tile_paraboloid_kernel(tc, inp, pars, out):
             nc.gpsimd.tensor_tensor(
                 out=p_term[:, col], in0=p0_half[:, col], in1=p_sq_half[:, col], op=ALU.subtract
             )
+
+        x_term_negative = consts.tile([P, X_BLOCKS], F32)
+        nc.gpsimd.tensor_scalar(
+            out=x_term_negative[:], in0=x_term[:], scalar1=-1.0, scalar2=0.0, op0=ALU.mult, op1=ALU.add
+        )
+
+        def store(j, first, end, out_sb):
+            nc.sync.dma_start(out=out_view[:, first:end, j * P : (j + 1) * P], in_=out_sb[:, first:end])
+
+        def finish(j, first, end, back):
+            out_sb = out_pool.tile([P, X_BLOCKS, P], F32)
+            blocks = end - first
+            nc.vector.scalar_tensor_tensor(
+                out=out_sb[:, first:end],
+                in0=back[:, first * P : end * P].rearrange("b (i m) -> b i m", i=blocks),
+                scalar=2.0 * OUTPUT_FACTOR,
+                in1=x_term[:, first:end].unsqueeze(2).to_broadcast([P, blocks, P]),
+                op0=ALU.mult,
+                op1=ALU.subtract,
+            )
+            store(j, first, end, out_sb)
+
+        def finish_on_scalar(j, back):
+            out_sb = out_pool.tile([P, X_BLOCKS, P], F32)
+            for i in range(X_BLOCKS):
+                nc.scalar.activation(
+                    out=out_sb[:, i],
+                    in_=back[:, i * P : (i + 1) * P],
+                    func=ACT.Identity,
+                    bias=x_term_negative[:, i : i + 1],
+                    scale=2.0 * OUTPUT_FACTOR,
+                )
+            store(j, 0, X_BLOCKS, out_sb)
+
+        def parts(j):
+            half = X_BLOCKS // 2
+            return [(0, half), (half, X_BLOCKS)] if j == PAIRS - 1 else [(0, X_BLOCKS)]
 
         words_h, words_p = {}, {}
         grouped_h, grouped_p = {}, {}
@@ -180,49 +230,48 @@ def tile_paraboloid_kernel(tc, inp, pars, out):
 
             j = r - COMBINE_LAG
             if 0 <= j < PAIRS:
-                u = work.tile([P, B], F32)
-                nc.vector.scalar_tensor_tensor(
-                    out=u[:],
-                    in0=product_p[j][:],
-                    scalar=p_term[:, j : j + 1],
-                    in1=half_square[j][:],
-                    op0=ALU.add,
-                    op1=ALU.add,
-                )
-                combined[j] = u
+                combined[j] = []
+                for first, end in parts(j):
+                    cols = slice(first * P, end * P)
+                    u = work.tile([P, B], F32)
+                    nc.vector.scalar_tensor_tensor(
+                        out=u[:, cols],
+                        in0=product_p[j][:, cols],
+                        scalar=p_term[:, j : j + 1],
+                        in1=half_square[j][:, cols],
+                        op0=ALU.add,
+                        op1=ALU.add,
+                    )
+                    combined[j].append(u)
 
+            if r == MULTIPLY_LAG:
+                keep_busy(2)
             if r < PAIRS:
                 words_h[r] = transpose_words(raw_h[r])
                 words_p[r] = transpose_words(raw_p[r])
             j = r - BACK_LAG
             if 0 <= j < PAIRS:
-                back = back_psum.tile([P, B], F32)
-                for i in range(X_BLOCKS):
-                    cols = slice(i * P, (i + 1) * P)
-                    nc.tensor.transpose(back[:, cols], combined[j][:, cols], identity[:])
+                backs = []
+                for (first, end), u in zip(parts(j), combined[j]):
+                    back = back_psum.tile([P, B], F32)
+                    for i in range(first, end):
+                        cols = slice(i * P, (i + 1) * P)
+                        nc.tensor.transpose(back[:, cols], u[:, cols], identity[:])
+                    backs.append(back)
 
             if r < PAIRS:
                 grouped_h[r] = regroup_block(nc.scalar.copy if r == 0 else nc.vector.tensor_copy, words_h[r])
                 grouped_p[r] = regroup_block(nc.scalar.copy, words_p[r])
 
-            if 0 <= j < PAIRS:
-                out_sb = out_pool.tile([P, X_BLOCKS, P], F32)
-                nc.vector.scalar_tensor_tensor(
-                    out=out_sb[:],
-                    in0=back[:].rearrange("b (i m) -> b i m", i=X_BLOCKS),
-                    scalar=2.0 * OUTPUT_FACTOR,
-                    in1=x_term[:].unsqueeze(2).to_broadcast([P, X_BLOCKS, P]),
-                    op0=ALU.mult,
-                    op1=ALU.subtract,
-                )
-                nc.sync.dma_start(out=out_view[:, :, j * P : (j + 1) * P], in_=out_sb[:])
+            if 0 <= j < PAIRS and j != PAIRS - 2:
+                for (first, end), back in zip(parts(j), backs):
+                    finish(j, first, end, back)
 
             if r < PAIRS:
                 mx_h[r] = quantise(grouped_h[r])
                 mx_p[r] = quantise(grouped_p[r])
             if r == 0:
-                nc.vector.tensor_scalar_mul(out=h0_bias[:], in0=bias_t[:, 0:PAIRS], scalar1=ROOT_HALF)
-                nc.vector.tensor_scalar_mul(out=p0_half[:], in0=bias_t[:, PAIRS : 2 * PAIRS], scalar1=0.5)
+                nc.vector.tensor_copy(out=bias_columns[:], in_=bias_t[:, 0 : 2 * PAIRS])
 
             j = r - MULTIPLY_LAG
             if 0 <= j < PAIRS:
@@ -236,6 +285,10 @@ def tile_paraboloid_kernel(tc, inp, pars, out):
                     out=s[:], in_=acc_h[:], func=ACT.Square, bias=h0_bias[:, j : j + 1], scale=ROOT_HALF
                 )
                 half_square[j] = s
+
+            j = r - BACK_LAG
+            if j == PAIRS - 2:
+                finish_on_scalar(j, backs[0])
 
             if r < PAIRS:
                 neuron_term(r)

@@ -49,15 +49,19 @@ def tile_paraboloid_kernel(tc, inp, pars, out):
         raw_pool = ctx.enter_context(tc.tile_pool(name="raw", bufs=2 * (PREFETCH + 1)))
         mx_pool = ctx.enter_context(tc.tile_pool(name="mx", bufs=6))
         work = ctx.enter_context(tc.tile_pool(name="work", bufs=2))
-        out_pool = ctx.enter_context(tc.tile_pool(name="out", bufs=4))
+        out_pool = ctx.enter_context(tc.tile_pool(name="out", bufs=3))
+        couple_pool = ctx.enter_context(tc.tile_pool(name="couple", bufs=3))
         words_psum = ctx.enter_context(tc.psum_pool(name="words_psum", bufs=4))
         acc_psum = ctx.enter_context(tc.psum_pool(name="acc_psum", bufs=1))
         back_psum = ctx.enter_context(tc.psum_pool(name="back_psum", bufs=2))
         ctx.enter_context(tc.manual_schedule())
 
-        def load_block(pool, rows):
+        def load_block(pool, rows, pieces=1):
             raw = pool.tile([P, D], BF16)
-            nc.sync.dma_start(out=raw[:], in_=rows)
+            width = D // pieces
+            for piece in range(pieces):
+                cols = slice(piece * width, (piece + 1) * width)
+                nc.sync.dma_start(out=raw[:, cols], in_=rows[:, cols])
             return raw
 
         def transpose_words(raw):
@@ -124,7 +128,7 @@ def tile_paraboloid_kernel(tc, inp, pars, out):
         nc.scalar.dma_start(out=bias_rows[0:PAIRS, :], in_=h0_rows)
         nc.scalar.dma_start(out=bias_rows[PAIRS : 2 * PAIRS, :], in_=p0_rows)
 
-        x_raw = [load_block(x_pool, x_blocks[i]) for i in range(X_BLOCKS)]
+        x_raw = [load_block(x_pool, x_blocks[i], pieces=2 if i == 0 else 1) for i in range(X_BLOCKS)]
         raw_h = {}
         raw_p = {}
         for j in range(PREFETCH):
@@ -189,18 +193,30 @@ def tile_paraboloid_kernel(tc, inp, pars, out):
         def store(j, first, end, out_sb):
             nc.sync.dma_start(out=out_view[:, first:end, j * P : (j + 1) * P], in_=out_sb[:, first:end])
 
+        couples = {}
+
         def finish(j, first, end, back):
-            out_sb = out_pool.tile([P, X_BLOCKS, P], F32)
+            if j >= PAIRS - 2:
+                out_sb = out_pool.tile([P, X_BLOCKS, P], F32)
+                target = out_sb[:, first:end]
+            else:
+                if j % 2 == 0:
+                    couples[j] = couple_pool.tile([P, X_BLOCKS, 2 * P], F32, name="couple")
+                out_sb = couples[j - j % 2]
+                target = out_sb[:, :, (j % 2) * P : (j % 2 + 1) * P]
             blocks = end - first
             nc.vector.scalar_tensor_tensor(
-                out=out_sb[:, first:end],
+                out=target,
                 in0=back[:, first * P : end * P].rearrange("b (i m) -> b i m", i=blocks),
                 scalar=2.0 * OUTPUT_FACTOR,
                 in1=x_term[:, first:end].unsqueeze(2).to_broadcast([P, blocks, P]),
                 op0=ALU.mult,
                 op1=ALU.subtract,
             )
-            store(j, first, end, out_sb)
+            if j >= PAIRS - 2:
+                store(j, first, end, out_sb)
+            elif j % 2 == 1:
+                nc.sync.dma_start(out=out_view[:, :, (j - 1) * P : (j + 1) * P], in_=out_sb[:])
 
         def finish_on_scalar(j, back):
             out_sb = out_pool.tile([P, X_BLOCKS, P], F32)

import math
from contextlib import ExitStack

import concourse.mybir as mybir
from concourse.masks import make_identity

BF16 = mybir.dt.bfloat16
F32 = mybir.dt.float32
U32 = mybir.dt.uint32
U8 = mybir.dt.uint8
FP8X4 = mybir.dt.float8_e4m3fn_x4
ALU = mybir.AluOpType
ACT = mybir.ActivationFunctionType

B, D, M = 512, 1024, 4096
INPUT_FACTOR = 0.01
OUTPUT_FACTOR = 0.1
FLOPS = 2 * 2 * B * D * M

P = 128
PACK = 4
PASSES = D // (P * PACK)
WORDS = D // 2
X_BLOCKS = B // P
PAIRS = M // P

ROOT_HALF = math.sqrt(0.5)
ROOT_OUTPUT_FACTOR = math.sqrt(OUTPUT_FACTOR)

MULTIPLY_LAG = 1
COMBINE_LAG = 2
BACK_LAG = 3
PREFETCH = 8


def tile_paraboloid_kernel(tc, inp, pars, out):
    nc = tc.nc

    h0_rows = pars[0:M].rearrange("(j m) -> j m", m=P)
    h_blocks = pars[M : M + M * D].rearrange("(j m k) -> j m k", m=P, k=D)
    p_blocks = pars[M + M * D : M + 2 * M * D].rearrange("(j m k) -> j m k", m=P, k=D)
    p0_rows = pars[M + 2 * M * D : 2 * M + 2 * M * D].rearrange("(j m) -> j m", m=P)
    x_blocks = inp.rearrange("(i b) k -> i b k", b=P)
    out_view = out.rearrange("(i b) m -> b i m", b=P)

    with ExitStack() as ctx:
        consts = ctx.enter_context(tc.tile_pool(name="consts", bufs=1))
        x_pool = ctx.enter_context(tc.tile_pool(name="x_raw", bufs=X_BLOCKS))
        raw_pool = ctx.enter_context(tc.tile_pool(name="raw", bufs=2 * (PREFETCH + 1)))
        mx_pool = ctx.enter_context(tc.tile_pool(name="mx", bufs=6))
        work = ctx.enter_context(tc.tile_pool(name="work", bufs=2))
        out_pool = ctx.enter_context(tc.tile_pool(name="out", bufs=3))
        couple_pool = ctx.enter_context(tc.tile_pool(name="couple", bufs=3))
        words_psum = ctx.enter_context(tc.psum_pool(name="words_psum", bufs=4))
        acc_psum = ctx.enter_context(tc.psum_pool(name="acc_psum", bufs=1))
        back_psum = ctx.enter_context(tc.psum_pool(name="back_psum", bufs=2))
        ctx.enter_context(tc.manual_schedule())

        def load_block(pool, rows, pieces=1):
            raw = pool.tile([P, D], BF16)
            width = D // pieces
            for piece in range(pieces):
                cols = slice(piece * width, (piece + 1) * width)
                nc.sync.dma_start(out=raw[:, cols], in_=rows[:, cols])
            return raw

        def transpose_words(raw):
            words_t = words_psum.tile([P, WORDS], F32)
            raw_words = raw[:].bitcast(F32)
            for c in range(WORDS // P):
                cols = slice(c * P, (c + 1) * P)
                nc.tensor.transpose(words_t[:, cols], raw_words[:, cols], identity[:])
            return words_t

        def regroup(copy, words_t, grouped_words):
            copy(out=grouped_words, in_=words_t[:].rearrange("q (g u r) -> q g r u", g=PASSES, u=2))

        def regroup_block(copy, words_t):
            grouped = mx_pool.tile([P, D], BF16, align_bytes=64)
            regroup(copy, words_t, grouped[:].bitcast(F32).rearrange("q (g r u) -> q g r u", g=PASSES, u=2))
            return grouped

        def quantise(grouped):
            codes = mx_pool.tile([P, D // PACK], U32, align_bytes=64)
            scales = mx_pool.tile([P, D // PACK], U8, align_bytes=64)
            nc.vector.quantize_mx(out=codes[:].bitcast(FP8X4), scales=scales[:], in_=grouped[:])
            return codes, scales

        def multiply(acc, codes, scales):
            for g in range(PASSES):
                w_cols = slice(g * P, (g + 1) * P)
                x_cols = slice(g * B, (g + 1) * B)
                nc.tensor.matmul_mx(
                    out=acc[:],
                    lhsT=codes[:, w_cols].bitcast(FP8X4),
                    lhsT_scale=scales[:, w_cols],
                    rhs=x_codes[:, x_cols].bitcast(FP8X4),
                    rhs_scale=x_scales[:, x_cols],
                    start=(g == 0),
                    stop=(g == PASSES - 1),
                )

        def sum_of_squares(raw, root_factor, total):
            squares = work.tile([P, D], BF16)
            nc.scalar.activation(
                out=squares[:], in_=raw[:], func=ACT.Square, scale=root_factor, accum_out=total
            )

        def sum_of_squares_on_vector(raw, factor, total):
            squares = work.tile([P, D], BF16)
            nc.vector.scalar_tensor_tensor(
                out=squares[:], in0=raw[:], scalar=factor, in1=raw[:], op0=ALU.mult, op1=ALU.mult, accum_out=total
            )

        identity = consts.tile([P, P], F32)
        make_identity(nc, identity[:])
        zeros = consts.tile([P, B], BF16)
        nc.vector.memset(zeros[:], 0.0)
        warm_bank = back_psum.tile([P, B], F32, tag="back")

        def keep_busy(count):
            for i in range(count):
                nc.tensor.matmul(warm_bank[:], zeros[:, 0:P], zeros[:], start=True, stop=True)

        keep_busy(4)

        bias_rows = consts.tile([P, P], BF16)
        nc.scalar.dma_start(out=bias_rows[0:PAIRS, :], in_=h0_rows)
        nc.scalar.dma_start(out=bias_rows[PAIRS : 2 * PAIRS, :], in_=p0_rows)

        x_raw = [load_block(x_pool, x_blocks[i], pieces=2 if i == 0 else 1) for i in range(X_BLOCKS)]
        raw_h = {}
        raw_p = {}
        for j in range(PREFETCH):
            raw_h[j] = load_block(raw_pool, h_blocks[j])
            raw_p[j] = load_block(raw_pool, p_blocks[j])

        bias_f32 = consts.tile([P, P], F32)
        nc.vector.memset(bias_f32[2 * PAIRS : P, :], 0.0)
        for rows, factor in ((slice(0, PAIRS), ROOT_HALF), (slice(PAIRS, 2 * PAIRS), 0.5)):
            nc.vector.tensor_scalar_mul(out=bias_f32[rows, :], in0=bias_rows[rows, :], scalar1=factor)

        x_term = consts.tile([P, X_BLOCKS], F32)
        x_grouped = consts.tile([P, PASSES * B * PACK], BF16, align_bytes=64)
        x_codes = consts.tile([P, PASSES * B], U32, align_bytes=64)
        x_scales = consts.tile([P, PASSES * B], U8, align_bytes=64)
        x_grouped_view = x_grouped[:].rearrange("q (g b u e) -> q g b u e", g=PASSES, u=2, e=2)

        for i in range(X_BLOCKS):
            if i == 0:
                sum_of_squares_on_vector(x_raw[i], OUTPUT_FACTOR * INPUT_FACTOR**2, x_term[:, i : i + 1])
            else:
                sum_of_squares(x_raw[i], INPUT_FACTOR * ROOT_OUTPUT_FACTOR, x_term[:, i : i + 1])
            words_t = transpose_words(x_raw[i])
            if i < X_BLOCKS - 1:
                keep_busy(1)
            for g in range(PASSES):
                nc.vector.tensor_scalar_mul(
                    out=x_grouped_view[:, g, i * P : (i + 1) * P],
                    in0=words_t[:].bitcast(BF16).rearrange("q (g u r e) -> q g r u e", g=PASSES, u=2, e=2)[:, g],
                    scalar1=INPUT_FACTOR,
                )

        bias_t = back_psum.tile([P, B], F32, tag="back")
        nc.tensor.transpose(bias_t[:, 0:P], bias_f32[:], identity[:])

        for g in range(PASSES):
            nc.vector.quantize_mx(
                out=x_codes[:, g * B : (g + 1) * B].bitcast(FP8X4),
                scales=x_scales[:, g * B : (g + 1) * B],
                in_=x_grouped[:, g * B * PACK : (g + 1) * B * PACK],
            )

        bias_columns = consts.tile([P, 2 * PAIRS], F32)
        h0_bias = bias_columns[:, 0:PAIRS]
        p0_half = bias_columns[:, PAIRS : 2 * PAIRS]

        p_sq_half = consts.tile([P, PAIRS], F32)
        p_term = consts.tile([P, PAIRS], F32)

        def neuron_term(j):
            col = slice(j, j + 1)
            sum_of_squares(raw_p[j], ROOT_HALF, p_sq_half[:, col])
            nc.gpsimd.tensor_tensor(
                out=p_term[:, col], in0=p0_half[:, col], in1=p_sq_half[:, col], op=ALU.subtract
            )

        x_term_negative = consts.tile([P, X_BLOCKS], F32)
        nc.gpsimd.tensor_scalar(
            out=x_term_negative[:], in0=x_term[:], scalar1=-1.0, scalar2=0.0, op0=ALU.mult, op1=ALU.add
        )

        def store(j, first, end, out_sb):
            nc.sync.dma_start(out=out_view[:, first:end, j * P : (j + 1) * P], in_=out_sb[:, first:end])

        couples = {}

        def finish(j, first, end, back):
            if j >= PAIRS - 2:
                out_sb = out_pool.tile([P, X_BLOCKS, P], F32)
                target = out_sb[:, first:end]
            else:
                if j % 2 == 0:
                    couples[j] = couple_pool.tile([P, X_BLOCKS, 2 * P], F32, name="couple")
                out_sb = couples[j - j % 2]
                target = out_sb[:, :, (j % 2) * P : (j % 2 + 1) * P]
            blocks = end - first
            nc.vector.scalar_tensor_tensor(
                out=target,
                in0=back[:, first * P : end * P].rearrange("b (i m) -> b i m", i=blocks),
                scalar=2.0 * OUTPUT_FACTOR,
                in1=x_term[:, first:end].unsqueeze(2).to_broadcast([P, blocks, P]),
                op0=ALU.mult,
                op1=ALU.subtract,
            )
            if j >= PAIRS - 2:
                store(j, first, end, out_sb)
            elif j % 2 == 1:
                nc.sync.dma_start(out=out_view[:, :, (j - 1) * P : (j + 1) * P], in_=out_sb[:])

        def finish_on_scalar(j, back):
            out_sb = out_pool.tile([P, X_BLOCKS, P], F32)
            for i in range(X_BLOCKS):
                nc.scalar.activation(
                    out=out_sb[:, i],
                    in_=back[:, i * P : (i + 1) * P],
                    func=ACT.Identity,
                    bias=x_term_negative[:, i : i + 1],
                    scale=2.0 * OUTPUT_FACTOR,
                )
            store(j, 0, X_BLOCKS, out_sb)

        def parts(j):
            half = X_BLOCKS // 2
            return [(0, half), (half, X_BLOCKS)] if j == PAIRS - 1 else [(0, X_BLOCKS)]

        words_h, words_p = {}, {}
        grouped_h, grouped_p = {}, {}
        mx_h, mx_p = {}, {}
        product_p, half_square, combined = {}, {}, {}

        for r in range(PAIRS + BACK_LAG):
            if r + PREFETCH < PAIRS:
                raw_h[r + PREFETCH] = load_block(raw_pool, h_blocks[r + PREFETCH])
                raw_p[r + PREFETCH] = load_block(raw_pool, p_blocks[r + PREFETCH])

            j = r - COMBINE_LAG
            if 0 <= j < PAIRS:
                combined[j] = []
                for first, end in parts(j):
                    cols = slice(first * P, end * P)
                    u = work.tile([P, B], F32)
                    nc.vector.scalar_tensor_tensor(
                        out=u[:, cols],
                        in0=product_p[j][:, cols],
                        scalar=p_term[:, j : j + 1],
                        in1=half_square[j][:, cols],
                        op0=ALU.add,
                        op1=ALU.add,
                    )
                    combined[j].append(u)

            if r == MULTIPLY_LAG:
                keep_busy(2)
            if r < PAIRS:
                words_h[r] = transpose_words(raw_h[r])
                words_p[r] = transpose_words(raw_p[r])
            j = r - BACK_LAG
            if 0 <= j < PAIRS:
                backs = []
                for (first, end), u in zip(parts(j), combined[j]):
                    back = back_psum.tile([P, B], F32)
                    for i in range(first, end):
                        cols = slice(i * P, (i + 1) * P)
                        nc.tensor.transpose(back[:, cols], u[:, cols], identity[:])
                    backs.append(back)

            if r < PAIRS:
                grouped_h[r] = regroup_block(nc.scalar.copy if r == 0 else nc.vector.tensor_copy, words_h[r])
                grouped_p[r] = regroup_block(nc.scalar.copy, words_p[r])

            if 0 <= j < PAIRS and j != PAIRS - 2:
                for (first, end), back in zip(parts(j), backs):
                    finish(j, first, end, back)

            if r < PAIRS:
                mx_h[r] = quantise(grouped_h[r])
                mx_p[r] = quantise(grouped_p[r])
            if r == 0:
                nc.vector.tensor_copy(out=bias_columns[:], in_=bias_t[:, 0 : 2 * PAIRS])

            j = r - MULTIPLY_LAG
            if 0 <= j < PAIRS:
                acc_h = acc_psum.tile([P, B], F32)
                acc_p = acc_psum.tile([P, B], F32)
                multiply(acc_h, mx_h[j][0], mx_h[j][1])
                multiply(acc_p, mx_p[j][0], mx_p[j][1])
                product_p[j] = acc_p
                s = work.tile([P, B], F32)
                nc.scalar.activation(
                    out=s[:], in_=acc_h[:], func=ACT.Square, bias=h0_bias[:, j : j + 1], scale=ROOT_HALF
                )
                half_square[j] = s

            j = r - BACK_LAG
            if j == PAIRS - 2:
                finish_on_scalar(j, backs[0])

            if r < PAIRS:
                neuron_term(r)
